import numpy as np
import ml_dtypes


def mxq(x, axis, fmt="e4m3"):
    dtype, down = {"e4m3": (ml_dtypes.float8_e4m3fn, 7), "e5m2": (ml_dtypes.float8_e5m2, 14)}[fmt]
    v = np.moveaxis(np.asarray(x, np.float32).astype(ml_dtypes.bfloat16).astype(np.float64), axis, -1)
    blocks = v.reshape(v.shape[:-1] + (-1, 32))
    amax = np.abs(blocks).max(-1, keepdims=True)
    byte = np.maximum(np.where(amax > 0, np.frexp(amax)[1] - 1 + 127, 0) - down, 1)
    scale = np.exp2(byte - 127.0)
    codes = (blocks / scale).astype(np.float32).astype(dtype).astype(np.float64)
    return np.moveaxis((codes * scale).reshape(v.shape), -1, axis)


WIDE = False


def mx_kscale(k):
    if not WIDE:
        return np.ones(k)
    levels = np.array([10, -10, 5, -5, 0])
    a = np.random.permutation(np.resize(levels, k // 512 * 4)).reshape(k // 512, 4)
    idx = np.arange(k)
    return np.exp2(a[idx // 512, idx % 128 // 32])


BF16 = ml_dtypes.bfloat16


def bf(x):
    return np.asarray(x, np.float32).astype(BF16)


def f64(x):
    return np.asarray(x).astype(np.float64)


E2M1 = np.array([0.0, 0.5, 1.0, 1.5, 2.0, 3.0, 4.0, 6.0, -0.0, -0.5, -1.0, -1.5, -2.0, -3.0, -4.0, -6.0])


def pack_weight(w, fmt):
    k, n = w.shape
    w = f64(bf(w)).reshape(k // 32, 32, n)
    amax = np.abs(w).max(1)
    if fmt == "e4m3":
        byte = np.frexp(amax)[1] - 1 + 127 - 7
    else:
        mant, ex = np.frexp(amax / 6.0)
        byte = np.where(mant > 0.5, ex, ex - 1) + 127
    byte = np.clip(np.where(amax > 0, byte, 1), 1, 254)
    scaled = (w * np.exp2(127.0 - byte)[:, None, :]).reshape(k, n).astype(np.float32)
    by_word = np.ascontiguousarray(scaled.reshape(k // 512, 128, 4, n).transpose(0, 1, 3, 2))
    if fmt == "e4m3":
        words = by_word.astype(ml_dtypes.float8_e4m3fn).view(np.uint8)
    else:
        c = by_word.astype(ml_dtypes.float4_e2m1fn).view(np.uint8) & 0xF
        words = c[..., 0::2] | (c[..., 1::2] << 4)
    return np.ascontiguousarray(words), np.ascontiguousarray(byte.astype(np.uint8).reshape(k // 512, 16, n))


def unpack_weight(words, scales, fmt):
    g, p, n, _ = words.shape
    if fmt == "e4m3":
        vals = np.ascontiguousarray(words).view(ml_dtypes.float8_e4m3fn).astype(np.float64)
    else:
        nib = np.empty((g, p, n, 4), np.uint8)
        nib[..., 0::2] = words & 0xF
        nib[..., 1::2] = words >> 4
        vals = E2M1[nib]
    vals = vals * np.repeat(np.exp2(scales.astype(np.float64) - 127.0), 8, axis=1)[..., None]
    return vals.transpose(0, 1, 3, 2).reshape(g * 512, n)


B, S, H, NH, NKV, HD = 2, 64, 16384, 32, 16, 32
ROPE_THETA = 10000.0
FMT = "e4m3"


def rope_tables():
    inv_freq = 1.0 / (ROPE_THETA ** (np.arange(0, HD, 2) / HD))
    pos = np.arange(S)[None, :] + np.random.randint(0, S, (B, 1))
    freqs = pos[:, :, None] * inv_freq[None, None, :]
    emb = np.concatenate([freqs, freqs], axis=-1)
    return np.cos(emb), np.sin(emb)


def rotate_half(x):
    x1, x2 = np.split(x, 2, axis=-1)
    return np.concatenate([-x2, x1], axis=-1)


def setup_inputs():
    s = mx_kscale(H)
    hidden_states = bf(np.random.standard_normal((B, S, H)) * s)
    q_w = np.random.standard_normal((NH * HD, H)) / np.sqrt(H) / s[None, :]
    k_w = np.random.standard_normal((NKV * HD, H)) / np.sqrt(H) / s[None, :]
    v_w = np.random.standard_normal((NKV * HD, H)) / np.sqrt(H) / s[None, :]
    q_w_words, q_w_scales = pack_weight(np.ascontiguousarray(q_w.T), FMT)
    k_w_words, k_w_scales = pack_weight(np.ascontiguousarray(k_w.T), FMT)
    v_w_words, v_w_scales = pack_weight(np.ascontiguousarray(v_w.T), FMT)
    cos, sin = rope_tables()
    return {"hidden_states": hidden_states, "cos": bf(cos), "sin": bf(sin), "q_w_words": q_w_words, "q_w_scales": q_w_scales, "k_w_words": k_w_words, "k_w_scales": k_w_scales, "v_w_words": v_w_words, "v_w_scales": v_w_scales}


def reference(hidden_states, cos, sin, q_w_words, q_w_scales, k_w_words, k_w_scales, v_w_words, v_w_scales):
    b, s, _ = hidden_states.shape
    xq = mxq(f64(hidden_states), 2, "e4m3")
    q = (xq @ unpack_weight(q_w_words, q_w_scales, FMT)).reshape(b, s, NH, HD).transpose(0, 2, 1, 3)
    k = (xq @ unpack_weight(k_w_words, k_w_scales, FMT)).reshape(b, s, NKV, HD).transpose(0, 2, 1, 3)
    v = (xq @ unpack_weight(v_w_words, v_w_scales, FMT)).reshape(b, s, NKV, HD).transpose(0, 2, 1, 3)
    c = f64(cos)[:, None, :, :]
    sn = f64(sin)[:, None, :, :]
    q = q * c + rotate_half(q) * sn
    k = k * c + rotate_half(k) * sn
    return (q, k, v)

@@ -1,0 +1,211 @@
+from contextlib import ExitStack
+
+import concourse.mybir as mybir
+from concourse.masks import make_identity
+
+F32 = mybir.dt.float32
+BF16 = mybir.dt.bfloat16
+I32 = mybir.dt.int32
+U32 = mybir.dt.uint32
+U8 = mybir.dt.uint8
+FP8X4 = mybir.dt.float8_e4m3fn_x4
+MULT = mybir.AluOpType.mult
+ADD = mybir.AluOpType.add
+
+P = 128
+BATCH = 2
+SEQ = 64
+K = 16384
+K_PASS = 512
+GROUPS = K // K_PASS
+HD = 32
+HALF = HD // 2
+N_BANK = 512
+HEADS_PER_BANK = N_BANK // HD
+
+X_CHUNKS = 4
+GROUPS_PER_CHUNK = GROUPS // X_CHUNKS
+CHUNK_K = K // X_CHUNKS
+GROUPS_PER_BANK = 2
+
+PLANES_PER_TILE = 4
+PLANE_BLOCKS = GROUPS // PLANES_PER_TILE
+
+LOAD_WORDS = 2048
+W_BUFS = 12
+
+FLOPS = 2 * P * K * 2048
+
+
+def load_scale_planes(nc, planes, scales):
+    by_row = scales.rearrange("(j c) q n -> q j c n", j=PLANES_PER_TILE)
+    for quadrant in range(4):
+        for r in range(4):
+            first = 32 * quadrant + r
+            nc.sync.dma_start(
+                out=planes[first : first + 4 * PLANES_PER_TILE : 4, :, :].bitcast(I32),
+                in_=by_row[4 * quadrant + r].bitcast(I32),
+            )
+
+
+def project(nc, w_pool, words, planes, x_codes, x_scales, banks):
+    n = words.shape[2]
+    groups_per_load = LOAD_WORDS // n
+    rows = words.rearrange("g p n t -> p g (n t)")
+    for first in range(0, GROUPS, groups_per_load):
+        w = w_pool.tile([P, groups_per_load, n], U32, tag="w", align_bytes=64)
+        nc.sync.dma_start(
+            out=w[:].bitcast(I32),
+            in_=rows[:, first : first + groups_per_load, :].bitcast(I32),
+        )
+        for i in range(groups_per_load):
+            g = first + i
+            offset = 4 * (g // PLANE_BLOCKS)
+            block = g % PLANE_BLOCKS
+            for b, acc in enumerate(banks):
+                cols = slice(b * N_BANK, (b + 1) * N_BANK)
+                nc.tensor.matmul_mx(
+                    out=acc[:],
+                    lhsT=x_codes[:, g, :].bitcast(FP8X4),
+                    lhsT_scale=x_scales[:, g, :],
+                    rhs=w[:, i, cols].bitcast(FP8X4),
+                    rhs_scale=planes[offset:P, block, cols],
+                    start=(g == 0),
+                    stop=(g == GROUPS - 1),
+                )
+
+
+def store_heads(queue, out, first_head, result):
+    for b in range(BATCH):
+        queue.dma_start(
+            out=out[b, first_head : first_head + HEADS_PER_BANK].rearrange("h s d -> s h d"),
+            in_=result[b * SEQ : (b + 1) * SEQ, :, :],
+        )
+
+
+def rotate(nc, work, acc, cos_bf, sin_signed):
+    y = acc[:].rearrange("p (h d) -> p h d", d=HD)
+    straight = work.tile([P, HEADS_PER_BANK, HD], F32)
+    turned = work.tile([P, HEADS_PER_BANK, HD], F32)
+    nc.vector.tensor_tensor(
+        out=straight[:],
+        in0=y,
+        in1=cos_bf[:].unsqueeze(1).to_broadcast([P, HEADS_PER_BANK, HD]),
+        op=MULT,
+    )
+    nc.vector.tensor_tensor(
+        out=turned[:, :, 0:HALF],
+        in0=y[:, :, HALF:HD],
+        in1=sin_signed[:, 0:HALF].unsqueeze(1).to_broadcast([P, HEADS_PER_BANK, HALF]),
+        op=MULT,
+    )
+    nc.vector.tensor_tensor(
+        out=turned[:, :, HALF:HD],
+        in0=y[:, :, 0:HALF],
+        in1=sin_signed[:, HALF:HD].unsqueeze(1).to_broadcast([P, HEADS_PER_BANK, HALF]),
+        op=MULT,
+    )
+    nc.vector.tensor_tensor(out=straight[:], in0=straight[:], in1=turned[:], op=ADD)
+    return straight
+
+
+def tile_mistralattention_k_kernel(
+    tc,
+    hidden_states,
+    cos,
+    sin,
+    q_w_words,
+    q_w_scales,
+    k_w_words,
+    k_w_scales,
+    v_w_words,
+    v_w_scales,
+    out_0,
+    out_1,
+    out_2,
+):
+    nc = tc.nc
+    with ExitStack() as ctx:
+        const = ctx.enter_context(tc.tile_pool(name="const", bufs=1))
+        x_pool = ctx.enter_context(tc.tile_pool(name="x", bufs=X_CHUNKS))
+        stage = ctx.enter_context(tc.tile_pool(name="stage", bufs=2))
+        w_pool = ctx.enter_context(tc.tile_pool(name="w", bufs=W_BUFS))
+        work = ctx.enter_context(tc.tile_pool(name="work", bufs=2))
+        xt_pool = ctx.enter_context(tc.psum_pool(name="xt", bufs=4))
+        acc_pool = ctx.enter_context(tc.psum_pool(name="acc", bufs=1))
+
+        q_planes = const.tile([P, PLANE_BLOCKS, 1024], U8, align_bytes=64)
+        k_planes = const.tile([P, PLANE_BLOCKS, 512], U8, align_bytes=64)
+        v_planes = const.tile([P, PLANE_BLOCKS, 512], U8, align_bytes=64)
+        for planes in (q_planes, k_planes, v_planes):
+            nc.vector.memset(planes[:].bitcast(I32), 0)
+
+        ident = const.tile([P, P], F32)
+        make_identity(nc, ident[:])
+
+        x_rows = hidden_states.rearrange("b s k -> (b s) k")
+        x_tiles = []
+        for c in range(X_CHUNKS):
+            x_sb = x_pool.tile([P, CHUNK_K], BF16)
+            nc.sync.dma_start(out=x_sb[:], in_=x_rows[:, c * CHUNK_K : (c + 1) * CHUNK_K])
+            x_tiles.append(x_sb)
+
+        cos_bf = const.tile([P, HD], BF16)
+        sin_bf = const.tile([P, HD], BF16)
+        nc.scalar.dma_start(out=cos_bf[:], in_=cos.rearrange("b s d -> (b s) d"))
+        nc.scalar.dma_start(out=sin_bf[:], in_=sin.rearrange("b s d -> (b s) d"))
+        sin_signed = const.tile([P, HD], BF16)
+        nc.vector.tensor_scalar_mul(out=sin_signed[:, 0:HALF], in0=sin_bf[:, 0:HALF], scalar1=-1.0)
+        nc.vector.tensor_copy(out=sin_signed[:, HALF:HD], in_=sin_bf[:, HALF:HD])
+
+        load_scale_planes(nc, q_planes, q_w_scales)
+
+        x_codes = const.tile([P, GROUPS, P], U32, align_bytes=64)
+        x_scales = const.tile([P, GROUPS, P], U8, align_bytes=64)
+        for c in range(X_CHUNKS):
+            x_words = x_tiles[c][:].bitcast(F32)
+            grouped = stage.tile([P, 4 * P * GROUPS_PER_CHUNK], BF16, align_bytes=64)
+            grouped_words = grouped[:].bitcast(F32)
+            for bank in range(GROUPS_PER_CHUNK // GROUPS_PER_BANK):
+                xt = xt_pool.tile([P, 2 * GROUPS_PER_BANK, P], F32)
+                for i in range(GROUPS_PER_BANK):
+                    first_word = (K_PASS // 2) * (bank * GROUPS_PER_BANK + i)
+                    for u in range(2):
+                        nc.tensor.transpose(
+                            xt[:, 2 * i + u, :],
+                            x_words[:, first_word + u : first_word + K_PASS // 2 : 2],
+                            ident[:],
+                        )
+                dst = grouped_words[:, bank * N_BANK : (bank + 1) * N_BANK].rearrange(
+                    "p (g r u) -> p g r u", g=GROUPS_PER_BANK, u=2
+                )
+                src = xt[:].rearrange("p (g u) r -> p g r u", u=2)
+                if bank % 2 == 0:
+                    nc.vector.tensor_copy(out=dst, in_=src)
+                else:
+                    nc.scalar.copy(out=dst, in_=src)
+            chunk_groups = slice(c * GROUPS_PER_CHUNK, (c + 1) * GROUPS_PER_CHUNK)
+            nc.vector.quantize_mx(
+                out=x_codes[:, chunk_groups, :].rearrange("p g r -> p (g r)").bitcast(FP8X4),
+                scales=x_scales[:, chunk_groups, :].rearrange("p g r -> p (g r)"),
+                in_=grouped[:],
+            )
+
+        acc_q0 = acc_pool.tile([P, N_BANK], F32)
+        acc_q1 = acc_pool.tile([P, N_BANK], F32)
+        acc_k = acc_pool.tile([P, N_BANK], F32)
+        acc_v = acc_pool.tile([P, N_BANK], F32)
+
+        project(nc, w_pool, q_w_words, q_planes, x_codes, x_scales, [acc_q0, acc_q1])
+        load_scale_planes(nc, k_planes, k_w_scales)
+        store_heads(nc.scalar, out_0, 0, rotate(nc, work, acc_q0, cos_bf, sin_signed))
+        store_heads(nc.scalar, out_0, HEADS_PER_BANK, rotate(nc, work, acc_q1, cos_bf, sin_signed))
+
+        project(nc, w_pool, k_w_words, k_planes, x_codes, x_scales, [acc_k])
+        load_scale_planes(nc, v_planes, v_w_scales)
+        store_heads(nc.scalar, out_1, 0, rotate(nc, work, acc_k, cos_bf, sin_signed))
+
+        project(nc, w_pool, v_w_words, v_planes, x_codes, x_scales, [acc_v])
+        v_out = work.tile([P, HEADS_PER_BANK, HD], F32)
+        nc.vector.tensor_copy(out=v_out[:], in_=acc_v[:].rearrange("p (h d) -> p h d", d=HD))
+        store_heads(nc.sync, out_2, 0, v_out)

@@ -32,7 +32,7 @@ PLANES_PER_TILE = 4
 PLANE_BLOCKS = GROUPS // PLANES_PER_TILE
 
 LOAD_WORDS = 2048
-W_BUFS = 12
+W_BUFS = 16
 
 FLOPS = 2 * P * K * 2048
 
@@ -42,9 +42,9 @@ def load_scale_planes(nc, planes, scales):
     for quadrant in range(4):
         for r in range(4):
             first = 32 * quadrant + r
-            nc.sync.dma_start(
-                out=planes[first : first + 4 * PLANES_PER_TILE : 4, :, :].bitcast(I32),
-                in_=by_row[4 * quadrant + r].bitcast(I32),
+            nc.gpsimd.dma_start(
+                out=planes[first : first + 4 * PLANES_PER_TILE : 4, :, :].bitcast(F32),
+                in_=by_row[4 * quadrant + r].bitcast(F32),
             )
 
 
@@ -159,6 +159,8 @@ def tile_mistralattention_k_kernel(
         nc.vector.tensor_copy(out=sin_signed[:, HALF:HD], in_=sin_bf[:, HALF:HD])
 
         load_scale_planes(nc, q_planes, q_w_scales)
+        load_scale_planes(nc, k_planes, k_w_scales)
+        load_scale_planes(nc, v_planes, v_w_scales)
 
         x_codes = const.tile([P, GROUPS, P], U32, align_bytes=64)
         x_scales = const.tile([P, GROUPS, P], U8, align_bytes=64)
@@ -197,12 +199,10 @@ def tile_mistralattention_k_kernel(
         acc_v = acc_pool.tile([P, N_BANK], F32)
 
         project(nc, w_pool, q_w_words, q_planes, x_codes, x_scales, [acc_q0, acc_q1])
-        load_scale_planes(nc, k_planes, k_w_scales)
         store_heads(nc.scalar, out_0, 0, rotate(nc, work, acc_q0, cos_bf, sin_signed))
         store_heads(nc.scalar, out_0, HEADS_PER_BANK, rotate(nc, work, acc_q1, cos_bf, sin_signed))
 
         project(nc, w_pool, k_w_words, k_planes, x_codes, x_scales, [acc_k])
-        load_scale_planes(nc, v_planes, v_w_scales)
         store_heads(nc.scalar, out_1, 0, rotate(nc, work, acc_k, cos_bf, sin_signed))
 
         project(nc, w_pool, v_w_words, v_planes, x_codes, x_scales, [acc_v])

@@ -33,6 +33,7 @@ PLANE_BLOCKS = GROUPS // PLANES_PER_TILE
 
 LOAD_WORDS = 2048
 W_BUFS = 16
+RESULT_BANKS = 4
 
 FLOPS = 2 * P * K * 2048
 
@@ -83,9 +84,9 @@ def store_heads(queue, out, first_head, result):
         )
 
 
-def rotate(nc, work, acc, cos_bf, sin_signed):
+def rotate(nc, results, work, acc, cos_bf, sin_signed):
     y = acc[:].rearrange("p (h d) -> p h d", d=HD)
-    straight = work.tile([P, HEADS_PER_BANK, HD], F32)
+    straight = results.tile([P, HEADS_PER_BANK, HD], F32, tag="result")
     turned = work.tile([P, HEADS_PER_BANK, HD], F32)
     nc.vector.tensor_tensor(
         out=straight[:],
@@ -131,8 +132,10 @@ def tile_mistralattention_k_kernel(
         stage = ctx.enter_context(tc.tile_pool(name="stage", bufs=2))
         w_pool = ctx.enter_context(tc.tile_pool(name="w", bufs=W_BUFS))
         work = ctx.enter_context(tc.tile_pool(name="work", bufs=2))
+        results = ctx.enter_context(tc.tile_pool(name="results", bufs=RESULT_BANKS))
         xt_pool = ctx.enter_context(tc.psum_pool(name="xt", bufs=4))
         acc_pool = ctx.enter_context(tc.psum_pool(name="acc", bufs=1))
+        ctx.enter_context(tc.manual_schedule())
 
         q_planes = const.tile([P, PLANE_BLOCKS, 1024], U8, align_bytes=64)
         k_planes = const.tile([P, PLANE_BLOCKS, 512], U8, align_bytes=64)
@@ -154,9 +157,6 @@ def tile_mistralattention_k_kernel(
         sin_bf = const.tile([P, HD], BF16)
         nc.scalar.dma_start(out=cos_bf[:], in_=cos.rearrange("b s d -> (b s) d"))
         nc.scalar.dma_start(out=sin_bf[:], in_=sin.rearrange("b s d -> (b s) d"))
-        sin_signed = const.tile([P, HD], BF16)
-        nc.vector.tensor_scalar_mul(out=sin_signed[:, 0:HALF], in0=sin_bf[:, 0:HALF], scalar1=-1.0)
-        nc.vector.tensor_copy(out=sin_signed[:, HALF:HD], in_=sin_bf[:, HALF:HD])
 
         load_scale_planes(nc, q_planes, q_w_scales)
         load_scale_planes(nc, k_planes, k_w_scales)
@@ -193,19 +193,25 @@ def tile_mistralattention_k_kernel(
                 in_=grouped[:],
             )
 
+        sin_signed = const.tile([P, HD], BF16)
+        nc.vector.tensor_scalar_mul(out=sin_signed[:, 0:HALF], in0=sin_bf[:, 0:HALF], scalar1=-1.0)
+        nc.vector.tensor_copy(out=sin_signed[:, HALF:HD], in_=sin_bf[:, HALF:HD])
+
         acc_q0 = acc_pool.tile([P, N_BANK], F32)
         acc_q1 = acc_pool.tile([P, N_BANK], F32)
         acc_k = acc_pool.tile([P, N_BANK], F32)
         acc_v = acc_pool.tile([P, N_BANK], F32)
 
         project(nc, w_pool, q_w_words, q_planes, x_codes, x_scales, [acc_q0, acc_q1])
-        store_heads(nc.scalar, out_0, 0, rotate(nc, work, acc_q0, cos_bf, sin_signed))
-        store_heads(nc.scalar, out_0, HEADS_PER_BANK, rotate(nc, work, acc_q1, cos_bf, sin_signed))
-
+        q0_out = rotate(nc, results, work, acc_q0, cos_bf, sin_signed)
+        q1_out = rotate(nc, results, work, acc_q1, cos_bf, sin_signed)
         project(nc, w_pool, k_w_words, k_planes, x_codes, x_scales, [acc_k])
-        store_heads(nc.scalar, out_1, 0, rotate(nc, work, acc_k, cos_bf, sin_signed))
-
+        k_out = rotate(nc, results, work, acc_k, cos_bf, sin_signed)
         project(nc, w_pool, v_w_words, v_planes, x_codes, x_scales, [acc_v])
-        v_out = work.tile([P, HEADS_PER_BANK, HD], F32)
+
+        store_heads(nc.sync, out_0, 0, q0_out)
+        store_heads(nc.sync, out_0, HEADS_PER_BANK, q1_out)
+        store_heads(nc.sync, out_1, 0, k_out)
+        v_out = results.tile([P, HEADS_PER_BANK, HD], F32, tag="result")
         nc.vector.tensor_copy(out=v_out[:], in_=acc_v[:].rearrange("p (h d) -> p h d", d=HD))
         store_heads(nc.sync, out_2, 0, v_out)

@@ -31,8 +31,8 @@ GROUPS_PER_BANK = 2
 PLANES_PER_TILE = 4
 PLANE_BLOCKS = GROUPS // PLANES_PER_TILE
 
-LOAD_WORDS = 2048
-W_BUFS = 16
+LOAD_WORDS = 1024
+W_BUFS = 32
 RESULT_BANKS = 4
 
 FLOPS = 2 * P * K * 2048

@@ -40,8 +40,8 @@ FLOPS = 2 * P * K * 2048
 
 def load_scale_planes(nc, planes, scales):
     by_row = scales.rearrange("(j c) q n -> q j c n", j=PLANES_PER_TILE)
-    for quadrant in range(4):
-        for r in range(4):
+    for r in range(4):
+        for quadrant in (0, 2, 1, 3):
             first = 32 * quadrant + r
             nc.gpsimd.dma_start(
                 out=planes[first : first + 4 * PLANES_PER_TILE : 4, :, :].bitcast(F32),

from contextlib import ExitStack

import concourse.mybir as mybir
from concourse.masks import make_identity

F32 = mybir.dt.float32
BF16 = mybir.dt.bfloat16
I32 = mybir.dt.int32
U32 = mybir.dt.uint32
U8 = mybir.dt.uint8
FP8X4 = mybir.dt.float8_e4m3fn_x4
MULT = mybir.AluOpType.mult
ADD = mybir.AluOpType.add

P = 128
BATCH = 2
SEQ = 64
K = 16384
K_PASS = 512
GROUPS = K // K_PASS
HD = 32
HALF = HD // 2
N_BANK = 512
HEADS_PER_BANK = N_BANK // HD

X_CHUNKS = 4
GROUPS_PER_CHUNK = GROUPS // X_CHUNKS
CHUNK_K = K // X_CHUNKS
GROUPS_PER_BANK = 2

PLANES_PER_TILE = 4
PLANE_BLOCKS = GROUPS // PLANES_PER_TILE

LOAD_WORDS = 1024
W_BUFS = 32
RESULT_BANKS = 4

FLOPS = 2 * P * K * 2048


def load_scale_planes(nc, planes, scales):
    by_row = scales.rearrange("(j c) q n -> q j c n", j=PLANES_PER_TILE)
    for r in range(4):
        for quadrant in (0, 2, 1, 3):
            first = 32 * quadrant + r
            nc.gpsimd.dma_start(
                out=planes[first : first + 4 * PLANES_PER_TILE : 4, :, :].bitcast(F32),
                in_=by_row[4 * quadrant + r].bitcast(F32),
            )


def project(nc, w_pool, words, planes, x_codes, x_scales, banks):
    n = words.shape[2]
    groups_per_load = LOAD_WORDS // n
    rows = words.rearrange("g p n t -> p g (n t)")
    for first in range(0, GROUPS, groups_per_load):
        w = w_pool.tile([P, groups_per_load, n], U32, tag="w", align_bytes=64)
        nc.sync.dma_start(
            out=w[:].bitcast(I32),
            in_=rows[:, first : first + groups_per_load, :].bitcast(I32),
        )
        for i in range(groups_per_load):
            g = first + i
            offset = 4 * (g // PLANE_BLOCKS)
            block = g % PLANE_BLOCKS
            for b, acc in enumerate(banks):
                cols = slice(b * N_BANK, (b + 1) * N_BANK)
                nc.tensor.matmul_mx(
                    out=acc[:],
                    lhsT=x_codes[:, g, :].bitcast(FP8X4),
                    lhsT_scale=x_scales[:, g, :],
                    rhs=w[:, i, cols].bitcast(FP8X4),
                    rhs_scale=planes[offset:P, block, cols],
                    start=(g == 0),
                    stop=(g == GROUPS - 1),
                )


def store_heads(queue, out, first_head, result):
    for b in range(BATCH):
        queue.dma_start(
            out=out[b, first_head : first_head + HEADS_PER_BANK].rearrange("h s d -> s h d"),
            in_=result[b * SEQ : (b + 1) * SEQ, :, :],
        )


def rotate(nc, results, work, acc, cos_bf, sin_signed):
    y = acc[:].rearrange("p (h d) -> p h d", d=HD)
    straight = results.tile([P, HEADS_PER_BANK, HD], F32, tag="result")
    turned = work.tile([P, HEADS_PER_BANK, HD], F32)
    nc.vector.tensor_tensor(
        out=straight[:],
        in0=y,
        in1=cos_bf[:].unsqueeze(1).to_broadcast([P, HEADS_PER_BANK, HD]),
        op=MULT,
    )
    nc.vector.tensor_tensor(
        out=turned[:, :, 0:HALF],
        in0=y[:, :, HALF:HD],
        in1=sin_signed[:, 0:HALF].unsqueeze(1).to_broadcast([P, HEADS_PER_BANK, HALF]),
        op=MULT,
    )
    nc.vector.tensor_tensor(
        out=turned[:, :, HALF:HD],
        in0=y[:, :, 0:HALF],
        in1=sin_signed[:, HALF:HD].unsqueeze(1).to_broadcast([P, HEADS_PER_BANK, HALF]),
        op=MULT,
    )
    nc.vector.tensor_tensor(out=straight[:], in0=straight[:], in1=turned[:], op=ADD)
    return straight


def tile_mistralattention_k_kernel(
    tc,
    hidden_states,
    cos,
    sin,
    q_w_words,
    q_w_scales,
    k_w_words,
    k_w_scales,
    v_w_words,
    v_w_scales,
    out_0,
    out_1,
    out_2,
):
    nc = tc.nc
    with ExitStack() as ctx:
        const = ctx.enter_context(tc.tile_pool(name="const", bufs=1))
        x_pool = ctx.enter_context(tc.tile_pool(name="x", bufs=X_CHUNKS))
        stage = ctx.enter_context(tc.tile_pool(name="stage", bufs=2))
        w_pool = ctx.enter_context(tc.tile_pool(name="w", bufs=W_BUFS))
        work = ctx.enter_context(tc.tile_pool(name="work", bufs=2))
        results = ctx.enter_context(tc.tile_pool(name="results", bufs=RESULT_BANKS))
        xt_pool = ctx.enter_context(tc.psum_pool(name="xt", bufs=4))
        acc_pool = ctx.enter_context(tc.psum_pool(name="acc", bufs=1))
        ctx.enter_context(tc.manual_schedule())

        q_planes = const.tile([P, PLANE_BLOCKS, 1024], U8, align_bytes=64)
        k_planes = const.tile([P, PLANE_BLOCKS, 512], U8, align_bytes=64)
        v_planes = const.tile([P, PLANE_BLOCKS, 512], U8, align_bytes=64)
        for planes in (q_planes, k_planes, v_planes):
            nc.vector.memset(planes[:].bitcast(I32), 0)

        ident = const.tile([P, P], F32)
        make_identity(nc, ident[:])

        x_rows = hidden_states.rearrange("b s k -> (b s) k")
        x_tiles = []
        for c in range(X_CHUNKS):
            x_sb = x_pool.tile([P, CHUNK_K], BF16)
            nc.sync.dma_start(out=x_sb[:], in_=x_rows[:, c * CHUNK_K : (c + 1) * CHUNK_K])
            x_tiles.append(x_sb)

        cos_bf = const.tile([P, HD], BF16)
        sin_bf = const.tile([P, HD], BF16)
        nc.scalar.dma_start(out=cos_bf[:], in_=cos.rearrange("b s d -> (b s) d"))
        nc.scalar.dma_start(out=sin_bf[:], in_=sin.rearrange("b s d -> (b s) d"))

        load_scale_planes(nc, q_planes, q_w_scales)
        load_scale_planes(nc, k_planes, k_w_scales)
        load_scale_planes(nc, v_planes, v_w_scales)

        x_codes = const.tile([P, GROUPS, P], U32, align_bytes=64)
        x_scales = const.tile([P, GROUPS, P], U8, align_bytes=64)
        for c in range(X_CHUNKS):
            x_words = x_tiles[c][:].bitcast(F32)
            grouped = stage.tile([P, 4 * P * GROUPS_PER_CHUNK], BF16, align_bytes=64)
            grouped_words = grouped[:].bitcast(F32)
            for bank in range(GROUPS_PER_CHUNK // GROUPS_PER_BANK):
                xt = xt_pool.tile([P, 2 * GROUPS_PER_BANK, P], F32)
                for i in range(GROUPS_PER_BANK):
                    first_word = (K_PASS // 2) * (bank * GROUPS_PER_BANK + i)
                    for u in range(2):
                        nc.tensor.transpose(
                            xt[:, 2 * i + u, :],
                            x_words[:, first_word + u : first_word + K_PASS // 2 : 2],
                            ident[:],
                        )
                dst = grouped_words[:, bank * N_BANK : (bank + 1) * N_BANK].rearrange(
                    "p (g r u) -> p g r u", g=GROUPS_PER_BANK, u=2
                )
                src = xt[:].rearrange("p (g u) r -> p g r u", u=2)
                if bank % 2 == 0:
                    nc.vector.tensor_copy(out=dst, in_=src)
                else:
                    nc.scalar.copy(out=dst, in_=src)
            chunk_groups = slice(c * GROUPS_PER_CHUNK, (c + 1) * GROUPS_PER_CHUNK)
            nc.vector.quantize_mx(
                out=x_codes[:, chunk_groups, :].rearrange("p g r -> p (g r)").bitcast(FP8X4),
                scales=x_scales[:, chunk_groups, :].rearrange("p g r -> p (g r)"),
                in_=grouped[:],
            )

        sin_signed = const.tile([P, HD], BF16)
        nc.vector.tensor_scalar_mul(out=sin_signed[:, 0:HALF], in0=sin_bf[:, 0:HALF], scalar1=-1.0)
        nc.vector.tensor_copy(out=sin_signed[:, HALF:HD], in_=sin_bf[:, HALF:HD])

        acc_q0 = acc_pool.tile([P, N_BANK], F32)
        acc_q1 = acc_pool.tile([P, N_BANK], F32)
        acc_k = acc_pool.tile([P, N_BANK], F32)
        acc_v = acc_pool.tile([P, N_BANK], F32)

        project(nc, w_pool, q_w_words, q_planes, x_codes, x_scales, [acc_q0, acc_q1])
        q0_out = rotate(nc, results, work, acc_q0, cos_bf, sin_signed)
        q1_out = rotate(nc, results, work, acc_q1, cos_bf, sin_signed)
        project(nc, w_pool, k_w_words, k_planes, x_codes, x_scales, [acc_k])
        k_out = rotate(nc, results, work, acc_k, cos_bf, sin_signed)
        project(nc, w_pool, v_w_words, v_planes, x_codes, x_scales, [acc_v])

        store_heads(nc.sync, out_0, 0, q0_out)
        store_heads(nc.sync, out_0, HEADS_PER_BANK, q1_out)
        store_heads(nc.sync, out_1, 0, k_out)
        v_out = results.tile([P, HEADS_PER_BANK, HD], F32, tag="result")
        nc.vector.tensor_copy(out=v_out[:], in_=acc_v[:].rearrange("p (h d) -> p h d", d=HD))
        store_heads(nc.sync, out_2, 0, v_out)
